import numpy as np
import ml_dtypes


def mxq(x, axis, fmt="e4m3"):
    dtype, down = {"e4m3": (ml_dtypes.float8_e4m3fn, 7), "e5m2": (ml_dtypes.float8_e5m2, 14)}[fmt]
    v = np.moveaxis(np.asarray(x, np.float32).astype(ml_dtypes.bfloat16).astype(np.float64), axis, -1)
    blocks = v.reshape(v.shape[:-1] + (-1, 32))
    amax = np.abs(blocks).max(-1, keepdims=True)
    byte = np.maximum(np.where(amax > 0, np.frexp(amax)[1] - 1 + 127, 0) - down, 1)
    scale = np.exp2(byte - 127.0)
    codes = (blocks / scale).astype(np.float32).astype(dtype).astype(np.float64)
    return np.moveaxis((codes * scale).reshape(v.shape), -1, axis)


WIDE = False


def mx_kscale(k):
    if not WIDE:
        return np.ones(k)
    levels = np.array([10, -10, 5, -5, 0])
    if k % 512:
        return np.exp2(np.random.permutation(np.resize(levels, k // 32))).repeat(32)
    a = np.empty((k // 512, 16))
    for p in range(k // 512):
        a[p, :8] = np.random.permutation(np.resize(levels, 8))
        for g in range(8):
            far = levels[np.abs(levels - a[p, g]) >= 10]
            a[p, g + 8] = far[np.random.randint(len(far))]
    return np.exp2(a.ravel()).repeat(32)


BF16 = ml_dtypes.bfloat16


def bf(x):
    return np.asarray(x, np.float32).astype(BF16)


def f64(x):
    return np.asarray(x).astype(np.float64)


B, IN, H, NS, SS, CS, NA = 6144, 256, 1024, 4, 4, 32, 3
NC = NS * CS


def setup_inputs():
    s = mx_kscale(H)
    return {
        "h": bf(np.tanh(np.random.standard_normal((B, H))) * s),
        "act_logits": bf(np.random.standard_normal((B, NS * NA)) * 1.5),
        "stacks": bf(np.random.standard_normal((B, NS, SS, CS)) * 1.5),
        "W_push": bf(np.random.standard_normal((NC, H)) * 5.0 / np.sqrt(H) / s),
        "b_push": bf(np.random.standard_normal(NC) * 0.7),
    }


def reference(h, act_logits, stacks, W_push, b_push):
    st = f64(stacks)
    push = ((mxq(f64(h), 1, "e4m3") @ mxq(f64(W_push), 1, "e4m3").T) + f64(b_push)).reshape(B, NS, CS)
    lg = f64(act_logits)
    e = np.exp(lg - lg.max(-1, keepdims=True))
    act = (e / e.sum(-1, keepdims=True)).reshape(B, NS, NA)
    pa, po, no = act[..., 0][..., None], act[..., 1][..., None], act[..., 2][..., None]
    top_new = pa * push + po * st[:, :, 1, :] + no * st[:, :, 0, :]
    zeros_tail = np.zeros((B, NS, 1, CS))
    pop_rest = np.concatenate([st[:, :, 2:, :], zeros_tail], axis=2)
    rest = (pa[:, :, :, None] * st[:, :, :-1, :]
            + po[:, :, :, None] * pop_rest
            + no[:, :, :, None] * st[:, :, 1:, :])
    return np.concatenate([top_new[:, :, None, :], rest], axis=2)

@@ -1,0 +1,275 @@
+from contextlib import ExitStack
+
+import concourse.mybir as mybir
+from concourse.masks import make_identity
+
+F32 = mybir.dt.float32
+BF16 = mybir.dt.bfloat16
+U32 = mybir.dt.uint32
+U8 = mybir.dt.uint8
+FP8X4 = mybir.dt.float8_e4m3fn_x4
+ALU = mybir.AluOpType
+ACT = mybir.ActivationFunctionType
+AX = mybir.AxisListType
+
+P = 128
+B, H, NS, SS, CS, NA = 6144, 1024, 4, 4, 32, 3
+STACK = SS * CS
+ROW = NS * STACK
+NL = NS * NA
+TILES = B // P
+PACK = 4
+PASSES = H // (P * PACK)
+WORDS = H // 2
+FLOPS = 2 * B * H * P
+
+SIZES = [1, 1, 1, 1] + [2] * 21 + [1, 1]
+CHUNKS = [1, 1, 2] + [4] * 11
+HEAD_TILES = 4
+LOAD_BUFS = 6
+O_BUFS = 5
+
+
+def tile_stackrnncore_pa_t_kernel(tc, h, act_logits, stacks, W_push, b_push, out):
+    nc = tc.nc
+    h_v = h.rearrange("(p t) k -> p (t k)", t=TILES)
+    st_v = stacks.rearrange("(p t) n i c -> p (t n i c)", t=TILES)
+    out_v = out.rearrange("(p t) n i c -> p (t n i c)", t=TILES)
+    lg_v = act_logits.rearrange("(p t) j -> p (t j)", t=TILES)
+
+    n_groups = len(SIZES)
+    n_chunks = len(CHUNKS)
+    g_start = [sum(SIZES[:g]) for g in range(n_groups)]
+    c_start = [sum(CHUNKS[:c]) for c in range(n_chunks)]
+    g_chunk = [max(c for c in range(n_chunks) if c_start[c] <= g_start[g]) for g in range(n_groups)]
+    c_first = [min(g for g in range(n_groups) if g_chunk[g] == c) for c in range(n_chunks)]
+    c_last = [max(g for g in range(n_groups) if g_chunk[g] == c) for c in range(n_chunks)]
+
+    with ExitStack() as ctx:
+        const = ctx.enter_context(tc.tile_pool(name="const", bufs=1))
+        hpool = ctx.enter_context(tc.tile_pool(name="hpool", bufs=LOAD_BUFS))
+        spool = ctx.enter_context(tc.tile_pool(name="spool", bufs=LOAD_BUFS))
+        opool = ctx.enter_context(tc.tile_pool(name="opool", bufs=O_BUFS))
+        gpool = ctx.enter_context(tc.tile_pool(name="gpool", bufs=2))
+        cpool = ctx.enter_context(tc.tile_pool(name="cpool", bufs=2))
+        upool = ctx.enter_context(tc.tile_pool(name="upool", bufs=2))
+        xt_ps = ctx.enter_context(tc.psum_pool(name="xt_ps", bufs=4))
+        acc_ps = ctx.enter_context(tc.psum_pool(name="acc_ps", bufs=2))
+        push_ps = ctx.enter_context(tc.psum_pool(name="push_ps", bufs=2))
+        ctx.enter_context(tc.manual_schedule())
+
+        x_tiles = {}
+        s_tiles = {}
+        o_tiles = {}
+        xt_tiles = {}
+        grp_tiles = {}
+        code_tiles = {}
+        acc_tiles = {}
+        sum_tiles = {}
+        push_tiles = {}
+
+        logits = const.tile([P, TILES * NL], BF16)
+        nc.sync.dma_start(out=logits[:], in_=lg_v)
+        w_sb = const.tile([P, H], BF16)
+        nc.sync.dma_start(out=w_sb[:], in_=W_push)
+        b_sb = const.tile([P, 1], BF16)
+        nc.sync.dma_start(out=b_sb[:], in_=b_push.rearrange("(p o) -> p o", o=1))
+
+        def load(c):
+            t0, ct = c_start[c], CHUNKS[c]
+            x_sb = hpool.tile([P, ct * H], BF16, tag="x", name="x_sb")
+            nc.sync.dma_start(out=x_sb[:], in_=h_v[:, t0 * H:(t0 + ct) * H])
+            s_sb = spool.tile([P, ct * ROW], BF16, tag="s", name="s_sb")
+            nc.sync.dma_start(out=s_sb[:], in_=st_v[:, t0 * ROW:(t0 + ct) * ROW])
+            x_tiles[c] = x_sb
+            s_tiles[c] = s_sb
+
+        for c in range(LOAD_BUFS):
+            load(c)
+
+        ident = const.tile([P, P], F32)
+        make_identity(nc, ident[:])
+
+        row_max = const.tile([P, TILES], F32)
+        shifted = const.tile([P, TILES * NL], F32)
+        expd = const.tile([P, TILES * NL], F32)
+        row_sum = const.tile([P, TILES], F32)
+        row_inv = const.tile([P, TILES], F32)
+        act = const.tile([P, TILES * NL], F32)
+
+        def by_row(values, ta, tb):
+            return values[:, ta * NL:tb * NL].rearrange("p (t j) -> p t j", j=NL)
+
+        def per_row(values, ta, tb):
+            return values[:, ta:tb].unsqueeze(2).to_broadcast([P, tb - ta, NL])
+
+        def softmax_max(ta, tb):
+            nc.vector.tensor_reduce(out=row_max[:, ta:tb], in_=by_row(logits, ta, tb), axis=AX.X, op=ALU.max)
+
+        def softmax_shift(ta, tb):
+            nc.vector.tensor_tensor(
+                out=by_row(shifted, ta, tb), in0=by_row(logits, ta, tb), in1=per_row(row_max, ta, tb), op=ALU.subtract
+            )
+
+        def softmax_exp(ta, tb):
+            nc.scalar.activation(out=expd[:, ta * NL:tb * NL], in_=shifted[:, ta * NL:tb * NL], func=ACT.Exp)
+
+        def softmax_norm(ta, tb):
+            nc.vector.tensor_reduce(out=row_sum[:, ta:tb], in_=by_row(expd, ta, tb), axis=AX.X, op=ALU.add)
+            nc.vector.reciprocal(out=row_inv[:, ta:tb], in_=row_sum[:, ta:tb])
+            nc.vector.tensor_tensor(
+                out=by_row(act, ta, tb), in0=by_row(expd, ta, tb), in1=per_row(row_inv, ta, tb), op=ALU.mult
+            )
+
+        def transpose_words(words, first_word):
+            xt = xt_ps.tile([P, PASSES, 2, P], F32, tag="xt", name="xt")
+            for m in range(PASSES):
+                for u in range(2):
+                    w0 = first_word + m * 2 * P
+                    nc.tensor.transpose(xt[:, m, u, :], words[:, w0 + u:w0 + 2 * P:2], ident[:])
+            return xt
+
+        def copy_out(xt, grouped_words):
+            nc.scalar.copy(out=grouped_words, in_=xt[:].rearrange("p m u r -> p m r u"))
+
+        def transposes(g):
+            c = g_chunk[g]
+            words = x_tiles[c][:].bitcast(F32)
+            for j in range(SIZES[g]):
+                xt_tiles[(g, j)] = transpose_words(words, (g_start[g] - c_start[c] + j) * WORDS)
+
+        def copies_out(g):
+            gt = SIZES[g]
+            grouped = gpool.tile([P, PASSES * gt * P * PACK], BF16, align_bytes=64, tag="grp", name="grouped")
+            gw = grouped[:].bitcast(F32).rearrange("p (m j r u) -> p m j r u", m=PASSES, j=gt, u=2)
+            for j in range(gt):
+                copy_out(xt_tiles[(g, j)], gw[:, :, j, :, :])
+            grp_tiles[g] = grouped
+
+        def quantise(g):
+            n_cols = SIZES[g] * P
+            codes = cpool.tile([P, PASSES * n_cols], U32, align_bytes=64, tag="codes", name="codes")
+            scales = cpool.tile([P, PASSES * n_cols], U8, align_bytes=64, tag="scales", name="scales")
+            nc.vector.quantize_mx(out=codes[:].bitcast(FP8X4), scales=scales[:], in_=grp_tiles[g][:])
+            code_tiles[g] = (codes, scales)
+
+        def mx_passes(g):
+            n_cols = SIZES[g] * P
+            codes, scales = code_tiles[g]
+            acc = acc_ps.tile([P, n_cols], F32, tag="acc", name="acc")
+            for m in range(PASSES):
+                nc.tensor.matmul_mx(
+                    out=acc[:],
+                    lhsT=w_codes[:, m * P:(m + 1) * P].bitcast(FP8X4),
+                    lhsT_scale=w_scales[:, m * P:(m + 1) * P],
+                    rhs=codes[:, m * n_cols:(m + 1) * n_cols].bitcast(FP8X4),
+                    rhs_scale=scales[:, m * n_cols:(m + 1) * n_cols],
+                    start=(m == 0),
+                    stop=(m == PASSES - 1),
+                )
+            acc_tiles[g] = acc
+
+        def add_bias(g):
+            sums = upool.tile([P, SIZES[g] * P], F32, tag="sums", name="sums")
+            nc.scalar.activation(out=sums[:], in_=acc_tiles[g][:], func=ACT.Identity, bias=bias[:, 0:1], scale=1.0)
+            sum_tiles[g] = sums
+
+        def back_transposes(g):
+            push = push_ps.tile([P, SIZES[g] * P], F32, tag="push", name="push")
+            for j in range(SIZES[g]):
+                nc.tensor.transpose(push[:, j * P:(j + 1) * P], sum_tiles[g][:, j * P:(j + 1) * P], ident[:])
+            push_tiles[g] = push
+
+        def stacks_of(g):
+            c = g_chunk[g]
+            entries = []
+            for q in range(SIZES[g] * NS):
+                lo = (g_start[g] - c_start[c]) * ROW + q * STACK
+                entries.append((q, s_tiles[c][:, lo:lo + STACK], o_tiles[c][:, lo:lo + STACK], g_start[g] * NL + q * NA))
+            return entries
+
+        def seed_lower_cells(g):
+            c = g_chunk[g]
+            if g == c_first[c]:
+                o_tiles[c] = opool.tile([P, CHUNKS[c] * ROW], F32, tag="o", name="o_sb")
+            for q, s_q, o_q, a_q in stacks_of(g):
+                nc.scalar.activation(
+                    out=o_q[:, CS:STACK], in_=s_q[:, 0:STACK - CS], func=ACT.Copy, scale=act[:, a_q:a_q + 1]
+                )
+
+        def seed_top_cells(g):
+            for q, s_q, o_q, a_q in stacks_of(g):
+                nc.scalar.activation(
+                    out=o_q[:, 0:CS], in_=push_tiles[g][:, q * CS:(q + 1) * CS], func=ACT.Copy, scale=act[:, a_q:a_q + 1]
+                )
+
+        def blend(g):
+            entries = stacks_of(g)
+            for j in range(SIZES[g]):
+                for q, s_q, o_q, a_q in entries[j * NS:(j + 1) * NS]:
+                    nc.vector.scalar_tensor_tensor(
+                        out=o_q, in0=s_q, scalar=act[:, a_q + 2:a_q + 3], in1=o_q, op0=ALU.mult, op1=ALU.add
+                    )
+                for q, s_q, o_q, a_q in entries[j * NS:(j + 1) * NS]:
+                    nc.vector.scalar_tensor_tensor(
+                        out=o_q[:, 0:STACK - CS],
+                        in0=s_q[:, CS:STACK],
+                        scalar=act[:, a_q + 1:a_q + 2],
+                        in1=o_q[:, 0:STACK - CS],
+                        op0=ALU.mult,
+                        op1=ALU.add,
+                    )
+
+        def store(g):
+            c = g_chunk[g]
+            t0, gt = g_start[g], SIZES[g]
+            if c == n_chunks - 1:
+                lo = (t0 - c_start[c]) * ROW
+                nc.sync.dma_start(out=out_v[:, t0 * ROW:(t0 + gt) * ROW], in_=o_tiles[c][:, lo:lo + gt * ROW])
+            elif g == c_last[c]:
+                nc.sync.dma_start(out=out_v[:, c_start[c] * ROW:(c_start[c] + CHUNKS[c]) * ROW], in_=o_tiles[c][:])
+            if g == c_last[c] and c + LOAD_BUFS < n_chunks:
+                load(c + LOAD_BUFS)
+
+        softmax_max(0, HEAD_TILES)
+        softmax_shift(0, HEAD_TILES)
+        softmax_exp(0, HEAD_TILES)
+        softmax_max(HEAD_TILES, TILES)
+        softmax_norm(0, HEAD_TILES)
+        softmax_shift(HEAD_TILES, TILES)
+
+        w_grouped = const.tile([P, PASSES * P * PACK], BF16, align_bytes=64)
+        copy_out(
+            transpose_words(w_sb[:].bitcast(F32), 0),
+            w_grouped[:].bitcast(F32).rearrange("p (m r u) -> p m r u", m=PASSES, u=2),
+        )
+        w_codes = const.tile([P, PASSES * P], U32, align_bytes=64)
+        w_scales = const.tile([P, PASSES * P], U8, align_bytes=64)
+        nc.vector.quantize_mx(out=w_codes[:].bitcast(FP8X4), scales=w_scales[:], in_=w_grouped[:])
+        bias = const.tile([P, 1], F32)
+        nc.vector.tensor_copy(out=bias[:], in_=b_sb[:])
+
+        for k in range(-3, n_groups):
+            if k >= 1:
+                store(k - 1)
+            if k + 3 < n_groups:
+                transposes(k + 3)
+            if 0 <= k + 1 < n_groups:
+                add_bias(k + 1)
+                back_transposes(k + 1)
+            if 0 <= k + 2 < n_groups:
+                quantise(k + 2)
+                mx_passes(k + 2)
+            if k == -2:
+                softmax_exp(HEAD_TILES, TILES)
+            if k == -1:
+                softmax_norm(HEAD_TILES, TILES)
+            if 0 <= k + 1 < n_groups:
+                seed_lower_cells(k + 1)
+            if k + 3 < n_groups:
+                copies_out(k + 3)
+            if 0 <= k + 1 < n_groups:
+                seed_top_cells(k + 1)
+            if k >= 0:
+                blend(k)
+        store(n_groups - 1)

@@ -193,9 +193,19 @@ def tile_stackrnncore_pa_t_kernel(tc, h, act_logits, stacks, W_push, b_push, out
             if g == c_first[c]:
                 o_tiles[c] = opool.tile([P, CHUNKS[c] * ROW], F32, tag="o", name="o_sb")
             for q, s_q, o_q, a_q in stacks_of(g):
-                nc.scalar.activation(
-                    out=o_q[:, CS:STACK], in_=s_q[:, 0:STACK - CS], func=ACT.Copy, scale=act[:, a_q:a_q + 1]
-                )
+                if g_start[g] < HEAD_TILES:
+                    nc.gpsimd.tensor_scalar(
+                        out=o_q[:, CS:STACK],
+                        in0=s_q[:, 0:STACK - CS],
+                        scalar1=act[:, a_q:a_q + 1],
+                        scalar2=0.0,
+                        op0=ALU.mult,
+                        op1=ALU.add,
+                    )
+                else:
+                    nc.scalar.activation(
+                        out=o_q[:, CS:STACK], in_=s_q[:, 0:STACK - CS], func=ACT.Copy, scale=act[:, a_q:a_q + 1]
+                    )
 
         def seed_top_cells(g):
             for q, s_q, o_q, a_q in stacks_of(g):

@@ -23,10 +23,11 @@ PASSES = H // (P * PACK)
 WORDS = H // 2
 FLOPS = 2 * B * H * P
 
-SIZES = [1, 1, 1, 1] + [2] * 21 + [1, 1]
-CHUNKS = [1, 1, 2] + [4] * 11
+SIZES = [1, 1] + [2] * 22 + [1, 1]
+CHUNKS = [1, 1, 2, 2, 2] + [4] * 10
 HEAD_TILES = 4
-LOAD_BUFS = 6
+GPSIMD_TILES = 6
+LOAD_BUFS = 8
 O_BUFS = 5
 
 
@@ -171,7 +172,7 @@ def tile_stackrnncore_pa_t_kernel(tc, h, act_logits, stacks, W_push, b_push, out
 
         def add_bias(g):
             sums = upool.tile([P, SIZES[g] * P], F32, tag="sums", name="sums")
-            nc.scalar.activation(out=sums[:], in_=acc_tiles[g][:], func=ACT.Identity, bias=bias[:, 0:1], scale=1.0)
+            nc.scalar.activation(out=sums[:], in_=acc_tiles[g][:], func=ACT.Identity, bias=b_sb[:, 0:1], scale=1.0)
             sum_tiles[g] = sums
 
         def back_transposes(g):
@@ -193,7 +194,7 @@ def tile_stackrnncore_pa_t_kernel(tc, h, act_logits, stacks, W_push, b_push, out
             if g == c_first[c]:
                 o_tiles[c] = opool.tile([P, CHUNKS[c] * ROW], F32, tag="o", name="o_sb")
             for q, s_q, o_q, a_q in stacks_of(g):
-                if g_start[g] < HEAD_TILES:
+                if g_start[g] < GPSIMD_TILES:
                     nc.gpsimd.tensor_scalar(
                         out=o_q[:, CS:STACK],
                         in0=s_q[:, 0:STACK - CS],
@@ -235,7 +236,13 @@ def tile_stackrnncore_pa_t_kernel(tc, h, act_logits, stacks, W_push, b_push, out
             t0, gt = g_start[g], SIZES[g]
             if c == n_chunks - 1:
                 lo = (t0 - c_start[c]) * ROW
-                nc.sync.dma_start(out=out_v[:, t0 * ROW:(t0 + gt) * ROW], in_=o_tiles[c][:, lo:lo + gt * ROW])
+                pieces = 2 if g == n_groups - 1 else 1
+                width = gt * ROW // pieces
+                for i in range(pieces):
+                    nc.sync.dma_start(
+                        out=out_v[:, t0 * ROW + i * width:t0 * ROW + (i + 1) * width],
+                        in_=o_tiles[c][:, lo + i * width:lo + (i + 1) * width],
+                    )
             elif g == c_last[c]:
                 nc.sync.dma_start(out=out_v[:, c_start[c] * ROW:(c_start[c] + CHUNKS[c]) * ROW], in_=o_tiles[c][:])
             if g == c_last[c] and c + LOAD_BUFS < n_chunks:
@@ -256,8 +263,6 @@ def tile_stackrnncore_pa_t_kernel(tc, h, act_logits, stacks, W_push, b_push, out
         w_codes = const.tile([P, PASSES * P], U32, align_bytes=64)
         w_scales = const.tile([P, PASSES * P], U8, align_bytes=64)
         nc.vector.quantize_mx(out=w_codes[:].bitcast(FP8X4), scales=w_scales[:], in_=w_grouped[:])
-        bias = const.tile([P, 1], F32)
-        nc.vector.tensor_copy(out=bias[:], in_=b_sb[:])
 
         for k in range(-3, n_groups):
             if k >= 1:

@@ -26,9 +26,9 @@ FLOPS = 2 * B * H * P
 SIZES = [1, 1] + [2] * 22 + [1, 1]
 CHUNKS = [1, 1, 2, 2, 2] + [4] * 10
 HEAD_TILES = 4
-GPSIMD_TILES = 6
+GPSIMD_TILES = 2
 LOAD_BUFS = 8
-O_BUFS = 5
+O_BUFS = 8
 
 
 def tile_stackrnncore_pa_t_kernel(tc, h, act_logits, stacks, W_push, b_push, out):

@@ -24,9 +24,10 @@ WORDS = H // 2
 FLOPS = 2 * B * H * P
 
 SIZES = [1, 1] + [2] * 22 + [1, 1]
+FIRST_PAIR = SIZES.index(2)
 CHUNKS = [1, 1, 2, 2, 2] + [4] * 10
 HEAD_TILES = 4
-GPSIMD_TILES = 2
+VECTOR_TILES = 2
 LOAD_BUFS = 8
 O_BUFS = 8
 
@@ -194,19 +195,32 @@ def tile_stackrnncore_pa_t_kernel(tc, h, act_logits, stacks, W_push, b_push, out
             if g == c_first[c]:
                 o_tiles[c] = opool.tile([P, CHUNKS[c] * ROW], F32, tag="o", name="o_sb")
             for q, s_q, o_q, a_q in stacks_of(g):
-                if g_start[g] < GPSIMD_TILES:
-                    nc.gpsimd.tensor_scalar(
+                if g_start[g] < VECTOR_TILES:
+                    nc.vector.tensor_scalar(
                         out=o_q[:, CS:STACK],
                         in0=s_q[:, 0:STACK - CS],
                         scalar1=act[:, a_q:a_q + 1],
-                        scalar2=0.0,
+                        scalar2=None,
                         op0=ALU.mult,
-                        op1=ALU.add,
                     )
                 else:
                     nc.scalar.activation(
                         out=o_q[:, CS:STACK], in_=s_q[:, 0:STACK - CS], func=ACT.Copy, scale=act[:, a_q:a_q + 1]
                     )
+
+        def seed_top_cells_together(g):
+            c = g_chunk[g]
+            lo = (g_start[g] - c_start[c]) * ROW
+            n_q = SIZES[g] * NS
+            cells = o_tiles[c][:, lo:lo + n_q * STACK].rearrange("p (q x) -> p q x", x=STACK)
+            a_lo = g_start[g] * NL
+            weights = act[:, a_lo:a_lo + n_q * NA].rearrange("p (q a) -> p q a", a=NA)
+            nc.vector.tensor_tensor(
+                out=cells[:, :, 0:CS],
+                in0=push_tiles[g][:].rearrange("p (q x) -> p q x", x=CS),
+                in1=weights[:, :, 0:1].to_broadcast([P, n_q, CS]),
+                op=ALU.mult,
+            )
 
         def seed_top_cells(g):
             for q, s_q, o_q, a_q in stacks_of(g):
@@ -273,18 +287,22 @@ def tile_stackrnncore_pa_t_kernel(tc, h, act_logits, stacks, W_push, b_push, out
                 add_bias(k + 1)
                 back_transposes(k + 1)
             if 0 <= k + 2 < n_groups:
+                if g_start[k + 2] < VECTOR_TILES:
+                    seed_lower_cells(k + 2)
                 quantise(k + 2)
                 mx_passes(k + 2)
             if k == -2:
                 softmax_exp(HEAD_TILES, TILES)
             if k == -1:
                 softmax_norm(HEAD_TILES, TILES)
-            if 0 <= k + 1 < n_groups:
+            if 0 <= k + 1 < n_groups and g_start[k + 1] >= VECTOR_TILES:
                 seed_lower_cells(k + 1)
             if k + 3 < n_groups:
                 copies_out(k + 3)
-            if 0 <= k + 1 < n_groups:
+            if 0 <= k + 1 < n_groups and k + 1 != FIRST_PAIR:
                 seed_top_cells(k + 1)
             if k >= 0:
                 blend(k)
+            if k + 1 == FIRST_PAIR:
+                seed_top_cells_together(k + 1)
         store(n_groups - 1)

@@ -55,6 +55,7 @@ def tile_stackrnncore_pa_t_kernel(tc, h, act_logits, stacks, W_push, b_push, out
         gpool = ctx.enter_context(tc.tile_pool(name="gpool", bufs=2))
         cpool = ctx.enter_context(tc.tile_pool(name="cpool", bufs=2))
         upool = ctx.enter_context(tc.tile_pool(name="upool", bufs=2))
+        epool = ctx.enter_context(tc.tile_pool(name="epool", bufs=3))
         xt_ps = ctx.enter_context(tc.psum_pool(name="xt_ps", bufs=4))
         acc_ps = ctx.enter_context(tc.psum_pool(name="acc_ps", bufs=2))
         push_ps = ctx.enter_context(tc.psum_pool(name="push_ps", bufs=2))
@@ -68,14 +69,13 @@ def tile_stackrnncore_pa_t_kernel(tc, h, act_logits, stacks, W_push, b_push, out
         code_tiles = {}
         acc_tiles = {}
         sum_tiles = {}
+        e_tiles = {}
         push_tiles = {}
 
         logits = const.tile([P, TILES * NL], BF16)
         nc.sync.dma_start(out=logits[:], in_=lg_v)
         w_sb = const.tile([P, H], BF16)
         nc.sync.dma_start(out=w_sb[:], in_=W_push)
-        b_sb = const.tile([P, 1], BF16)
-        nc.sync.dma_start(out=b_sb[:], in_=b_push.rearrange("(p o) -> p o", o=1))
 
         def load(c):
             t0, ct = c_start[c], CHUNKS[c]
@@ -86,7 +86,10 @@ def tile_stackrnncore_pa_t_kernel(tc, h, act_logits, stacks, W_push, b_push, out
             x_tiles[c] = x_sb
             s_tiles[c] = s_sb
 
-        for c in range(LOAD_BUFS):
+        load(0)
+        b_sb = const.tile([P, 1], BF16)
+        nc.sync.dma_start(out=b_sb[:], in_=b_push.rearrange("(p o) -> p o", o=1))
+        for c in range(1, LOAD_BUFS):
             load(c)
 
         ident = const.tile([P, P], F32)
@@ -187,17 +190,19 @@ def tile_stackrnncore_pa_t_kernel(tc, h, act_logits, stacks, W_push, b_push, out
             entries = []
             for q in range(SIZES[g] * NS):
                 lo = (g_start[g] - c_start[c]) * ROW + q * STACK
-                entries.append((q, s_tiles[c][:, lo:lo + STACK], o_tiles[c][:, lo:lo + STACK], g_start[g] * NL + q * NA))
+                s_q, o_q = s_tiles[c][:, lo:lo + STACK], o_tiles[c][:, lo:lo + STACK]
+                entries.append((q, s_q, o_q, e_tiles[g][:, q * STACK:(q + 1) * STACK], g_start[g] * NL + q * NA))
             return entries
 
         def seed_lower_cells(g):
             c = g_chunk[g]
             if g == c_first[c]:
                 o_tiles[c] = opool.tile([P, CHUNKS[c] * ROW], F32, tag="o", name="o_sb")
-            for q, s_q, o_q, a_q in stacks_of(g):
+            e_tiles[g] = epool.tile([P, SIZES[g] * ROW], F32, tag="e", name="e_sb")
+            for q, s_q, o_q, e_q, a_q in stacks_of(g):
                 if g_start[g] < VECTOR_TILES:
                     nc.vector.tensor_scalar(
-                        out=o_q[:, CS:STACK],
+                        out=e_q[:, CS:STACK],
                         in0=s_q[:, 0:STACK - CS],
                         scalar1=act[:, a_q:a_q + 1],
                         scalar2=None,
@@ -205,14 +210,12 @@ def tile_stackrnncore_pa_t_kernel(tc, h, act_logits, stacks, W_push, b_push, out
                     )
                 else:
                     nc.scalar.activation(
-                        out=o_q[:, CS:STACK], in_=s_q[:, 0:STACK - CS], func=ACT.Copy, scale=act[:, a_q:a_q + 1]
+                        out=e_q[:, CS:STACK], in_=s_q[:, 0:STACK - CS], func=ACT.Copy, scale=act[:, a_q:a_q + 1]
                     )
 
         def seed_top_cells_together(g):
-            c = g_chunk[g]
-            lo = (g_start[g] - c_start[c]) * ROW
             n_q = SIZES[g] * NS
-            cells = o_tiles[c][:, lo:lo + n_q * STACK].rearrange("p (q x) -> p q x", x=STACK)
+            cells = e_tiles[g][:].rearrange("p (q x) -> p q x", x=STACK)
             a_lo = g_start[g] * NL
             weights = act[:, a_lo:a_lo + n_q * NA].rearrange("p (q a) -> p q a", a=NA)
             nc.vector.tensor_tensor(
@@ -223,19 +226,19 @@ def tile_stackrnncore_pa_t_kernel(tc, h, act_logits, stacks, W_push, b_push, out
             )
 
         def seed_top_cells(g):
-            for q, s_q, o_q, a_q in stacks_of(g):
+            for q, s_q, o_q, e_q, a_q in stacks_of(g):
                 nc.scalar.activation(
-                    out=o_q[:, 0:CS], in_=push_tiles[g][:, q * CS:(q + 1) * CS], func=ACT.Copy, scale=act[:, a_q:a_q + 1]
+                    out=e_q[:, 0:CS], in_=push_tiles[g][:, q * CS:(q + 1) * CS], func=ACT.Copy, scale=act[:, a_q:a_q + 1]
                 )
 
         def blend(g):
             entries = stacks_of(g)
             for j in range(SIZES[g]):
-                for q, s_q, o_q, a_q in entries[j * NS:(j + 1) * NS]:
+                for q, s_q, o_q, e_q, a_q in entries[j * NS:(j + 1) * NS]:
                     nc.vector.scalar_tensor_tensor(
-                        out=o_q, in0=s_q, scalar=act[:, a_q + 2:a_q + 3], in1=o_q, op0=ALU.mult, op1=ALU.add
+                        out=o_q, in0=s_q, scalar=act[:, a_q + 2:a_q + 3], in1=e_q, op0=ALU.mult, op1=ALU.add
                     )
-                for q, s_q, o_q, a_q in entries[j * NS:(j + 1) * NS]:
+                for q, s_q, o_q, e_q, a_q in entries[j * NS:(j + 1) * NS]:
                     nc.vector.scalar_tensor_tensor(
                         out=o_q[:, 0:STACK - CS],
                         in0=s_q[:, CS:STACK],

@@ -74,13 +74,21 @@ def tile_stackrnncore_pa_t_kernel(tc, h, act_logits, stacks, W_push, b_push, out
 
         logits = const.tile([P, TILES * NL], BF16)
         nc.sync.dma_start(out=logits[:], in_=lg_v)
+        half = H // PASSES
         w_sb = const.tile([P, H], BF16)
-        nc.sync.dma_start(out=w_sb[:], in_=W_push)
+        for m in range(PASSES):
+            nc.sync.dma_start(out=w_sb[:, m * half:(m + 1) * half], in_=W_push[:, m * half:(m + 1) * half])
 
         def load(c):
             t0, ct = c_start[c], CHUNKS[c]
             x_sb = hpool.tile([P, ct * H], BF16, tag="x", name="x_sb")
-            nc.sync.dma_start(out=x_sb[:], in_=h_v[:, t0 * H:(t0 + ct) * H])
+            pieces = PASSES if c == 0 else 1
+            width = ct * H // pieces
+            for i in range(pieces):
+                nc.sync.dma_start(
+                    out=x_sb[:, i * width:(i + 1) * width],
+                    in_=h_v[:, t0 * H + i * width:t0 * H + (i + 1) * width],
+                )
             s_sb = spool.tile([P, ct * ROW], BF16, tag="s", name="s_sb")
             nc.sync.dma_start(out=s_sb[:], in_=st_v[:, t0 * ROW:(t0 + ct) * ROW])
             x_tiles[c] = x_sb
@@ -119,8 +127,10 @@ def tile_stackrnncore_pa_t_kernel(tc, h, act_logits, stacks, W_push, b_push, out
         def softmax_exp(ta, tb):
             nc.scalar.activation(out=expd[:, ta * NL:tb * NL], in_=shifted[:, ta * NL:tb * NL], func=ACT.Exp)
 
-        def softmax_norm(ta, tb):
+        def softmax_sum(ta, tb):
             nc.vector.tensor_reduce(out=row_sum[:, ta:tb], in_=by_row(expd, ta, tb), axis=AX.X, op=ALU.add)
+
+        def softmax_norm(ta, tb):
             nc.vector.reciprocal(out=row_inv[:, ta:tb], in_=row_sum[:, ta:tb])
             nc.vector.tensor_tensor(
                 out=by_row(act, ta, tb), in0=by_row(expd, ta, tb), in1=per_row(row_inv, ta, tb), op=ALU.mult
@@ -269,6 +279,7 @@ def tile_stackrnncore_pa_t_kernel(tc, h, act_logits, stacks, W_push, b_push, out
         softmax_shift(0, HEAD_TILES)
         softmax_exp(0, HEAD_TILES)
         softmax_max(HEAD_TILES, TILES)
+        softmax_sum(0, HEAD_TILES)
         softmax_norm(0, HEAD_TILES)
         softmax_shift(HEAD_TILES, TILES)
 
@@ -289,6 +300,8 @@ def tile_stackrnncore_pa_t_kernel(tc, h, act_logits, stacks, W_push, b_push, out
             if 0 <= k + 1 < n_groups:
                 add_bias(k + 1)
                 back_transposes(k + 1)
+            if k == -1:
+                softmax_sum(HEAD_TILES, TILES)
             if 0 <= k + 2 < n_groups:
                 if g_start[k + 2] < VECTOR_TILES:
                     seed_lower_cells(k + 2)
@@ -298,10 +311,10 @@ def tile_stackrnncore_pa_t_kernel(tc, h, act_logits, stacks, W_push, b_push, out
                 softmax_exp(HEAD_TILES, TILES)
             if k == -1:
                 softmax_norm(HEAD_TILES, TILES)
-            if 0 <= k + 1 < n_groups and g_start[k + 1] >= VECTOR_TILES:
-                seed_lower_cells(k + 1)
             if k + 3 < n_groups:
                 copies_out(k + 3)
+            if 0 <= k + 1 < n_groups and g_start[k + 1] >= VECTOR_TILES:
+                seed_lower_cells(k + 1)
             if 0 <= k + 1 < n_groups and k + 1 != FIRST_PAIR:
                 seed_top_cells(k + 1)
             if k >= 0:

from contextlib import ExitStack

import concourse.mybir as mybir
from concourse.masks import make_identity

F32 = mybir.dt.float32
BF16 = mybir.dt.bfloat16
U32 = mybir.dt.uint32
U8 = mybir.dt.uint8
FP8X4 = mybir.dt.float8_e4m3fn_x4
ALU = mybir.AluOpType
ACT = mybir.ActivationFunctionType
AX = mybir.AxisListType

P = 128
B, H, NS, SS, CS, NA = 6144, 1024, 4, 4, 32, 3
STACK = SS * CS
ROW = NS * STACK
NL = NS * NA
TILES = B // P
PACK = 4
PASSES = H // (P * PACK)
WORDS = H // 2
FLOPS = 2 * B * H * P

SIZES = [1, 1] + [2] * 22 + [1, 1]
FIRST_PAIR = SIZES.index(2)
CHUNKS = [1, 1, 2, 2, 2] + [4] * 10
HEAD_TILES = 4
VECTOR_TILES = 2
LOAD_BUFS = 8
O_BUFS = 8


def tile_stackrnncore_pa_t_kernel(tc, h, act_logits, stacks, W_push, b_push, out):
    nc = tc.nc
    h_v = h.rearrange("(p t) k -> p (t k)", t=TILES)
    st_v = stacks.rearrange("(p t) n i c -> p (t n i c)", t=TILES)
    out_v = out.rearrange("(p t) n i c -> p (t n i c)", t=TILES)
    lg_v = act_logits.rearrange("(p t) j -> p (t j)", t=TILES)

    n_groups = len(SIZES)
    n_chunks = len(CHUNKS)
    g_start = [sum(SIZES[:g]) for g in range(n_groups)]
    c_start = [sum(CHUNKS[:c]) for c in range(n_chunks)]
    g_chunk = [max(c for c in range(n_chunks) if c_start[c] <= g_start[g]) for g in range(n_groups)]
    c_first = [min(g for g in range(n_groups) if g_chunk[g] == c) for c in range(n_chunks)]
    c_last = [max(g for g in range(n_groups) if g_chunk[g] == c) for c in range(n_chunks)]

    with ExitStack() as ctx:
        const = ctx.enter_context(tc.tile_pool(name="const", bufs=1))
        hpool = ctx.enter_context(tc.tile_pool(name="hpool", bufs=LOAD_BUFS))
        spool = ctx.enter_context(tc.tile_pool(name="spool", bufs=LOAD_BUFS))
        opool = ctx.enter_context(tc.tile_pool(name="opool", bufs=O_BUFS))
        gpool = ctx.enter_context(tc.tile_pool(name="gpool", bufs=2))
        cpool = ctx.enter_context(tc.tile_pool(name="cpool", bufs=2))
        upool = ctx.enter_context(tc.tile_pool(name="upool", bufs=2))
        epool = ctx.enter_context(tc.tile_pool(name="epool", bufs=3))
        xt_ps = ctx.enter_context(tc.psum_pool(name="xt_ps", bufs=4))
        acc_ps = ctx.enter_context(tc.psum_pool(name="acc_ps", bufs=2))
        push_ps = ctx.enter_context(tc.psum_pool(name="push_ps", bufs=2))
        ctx.enter_context(tc.manual_schedule())

        x_tiles = {}
        s_tiles = {}
        o_tiles = {}
        xt_tiles = {}
        grp_tiles = {}
        code_tiles = {}
        acc_tiles = {}
        sum_tiles = {}
        e_tiles = {}
        push_tiles = {}

        logits = const.tile([P, TILES * NL], BF16)
        nc.sync.dma_start(out=logits[:], in_=lg_v)
        half = H // PASSES
        w_sb = const.tile([P, H], BF16)
        for m in range(PASSES):
            nc.sync.dma_start(out=w_sb[:, m * half:(m + 1) * half], in_=W_push[:, m * half:(m + 1) * half])

        def load(c):
            t0, ct = c_start[c], CHUNKS[c]
            x_sb = hpool.tile([P, ct * H], BF16, tag="x", name="x_sb")
            pieces = PASSES if c == 0 else 1
            width = ct * H // pieces
            for i in range(pieces):
                nc.sync.dma_start(
                    out=x_sb[:, i * width:(i + 1) * width],
                    in_=h_v[:, t0 * H + i * width:t0 * H + (i + 1) * width],
                )
            s_sb = spool.tile([P, ct * ROW], BF16, tag="s", name="s_sb")
            nc.sync.dma_start(out=s_sb[:], in_=st_v[:, t0 * ROW:(t0 + ct) * ROW])
            x_tiles[c] = x_sb
            s_tiles[c] = s_sb

        load(0)
        b_sb = const.tile([P, 1], BF16)
        nc.sync.dma_start(out=b_sb[:], in_=b_push.rearrange("(p o) -> p o", o=1))
        for c in range(1, LOAD_BUFS):
            load(c)

        ident = const.tile([P, P], F32)
        make_identity(nc, ident[:])

        row_max = const.tile([P, TILES], F32)
        shifted = const.tile([P, TILES * NL], F32)
        expd = const.tile([P, TILES * NL], F32)
        row_sum = const.tile([P, TILES], F32)
        row_inv = const.tile([P, TILES], F32)
        act = const.tile([P, TILES * NL], F32)

        def by_row(values, ta, tb):
            return values[:, ta * NL:tb * NL].rearrange("p (t j) -> p t j", j=NL)

        def per_row(values, ta, tb):
            return values[:, ta:tb].unsqueeze(2).to_broadcast([P, tb - ta, NL])

        def softmax_max(ta, tb):
            nc.vector.tensor_reduce(out=row_max[:, ta:tb], in_=by_row(logits, ta, tb), axis=AX.X, op=ALU.max)

        def softmax_shift(ta, tb):
            nc.vector.tensor_tensor(
                out=by_row(shifted, ta, tb), in0=by_row(logits, ta, tb), in1=per_row(row_max, ta, tb), op=ALU.subtract
            )

        def softmax_exp(ta, tb):
            nc.scalar.activation(out=expd[:, ta * NL:tb * NL], in_=shifted[:, ta * NL:tb * NL], func=ACT.Exp)

        def softmax_sum(ta, tb):
            nc.vector.tensor_reduce(out=row_sum[:, ta:tb], in_=by_row(expd, ta, tb), axis=AX.X, op=ALU.add)

        def softmax_norm(ta, tb):
            nc.vector.reciprocal(out=row_inv[:, ta:tb], in_=row_sum[:, ta:tb])
            nc.vector.tensor_tensor(
                out=by_row(act, ta, tb), in0=by_row(expd, ta, tb), in1=per_row(row_inv, ta, tb), op=ALU.mult
            )

        def transpose_words(words, first_word):
            xt = xt_ps.tile([P, PASSES, 2, P], F32, tag="xt", name="xt")
            for m in range(PASSES):
                for u in range(2):
                    w0 = first_word + m * 2 * P
                    nc.tensor.transpose(xt[:, m, u, :], words[:, w0 + u:w0 + 2 * P:2], ident[:])
            return xt

        def copy_out(xt, grouped_words):
            nc.scalar.copy(out=grouped_words, in_=xt[:].rearrange("p m u r -> p m r u"))

        def transposes(g):
            c = g_chunk[g]
            words = x_tiles[c][:].bitcast(F32)
            for j in range(SIZES[g]):
                xt_tiles[(g, j)] = transpose_words(words, (g_start[g] - c_start[c] + j) * WORDS)

        def copies_out(g):
            gt = SIZES[g]
            grouped = gpool.tile([P, PASSES * gt * P * PACK], BF16, align_bytes=64, tag="grp", name="grouped")
            gw = grouped[:].bitcast(F32).rearrange("p (m j r u) -> p m j r u", m=PASSES, j=gt, u=2)
            for j in range(gt):
                copy_out(xt_tiles[(g, j)], gw[:, :, j, :, :])
            grp_tiles[g] = grouped

        def quantise(g):
            n_cols = SIZES[g] * P
            codes = cpool.tile([P, PASSES * n_cols], U32, align_bytes=64, tag="codes", name="codes")
            scales = cpool.tile([P, PASSES * n_cols], U8, align_bytes=64, tag="scales", name="scales")
            nc.vector.quantize_mx(out=codes[:].bitcast(FP8X4), scales=scales[:], in_=grp_tiles[g][:])
            code_tiles[g] = (codes, scales)

        def mx_passes(g):
            n_cols = SIZES[g] * P
            codes, scales = code_tiles[g]
            acc = acc_ps.tile([P, n_cols], F32, tag="acc", name="acc")
            for m in range(PASSES):
                nc.tensor.matmul_mx(
                    out=acc[:],
                    lhsT=w_codes[:, m * P:(m + 1) * P].bitcast(FP8X4),
                    lhsT_scale=w_scales[:, m * P:(m + 1) * P],
                    rhs=codes[:, m * n_cols:(m + 1) * n_cols].bitcast(FP8X4),
                    rhs_scale=scales[:, m * n_cols:(m + 1) * n_cols],
                    start=(m == 0),
                    stop=(m == PASSES - 1),
                )
            acc_tiles[g] = acc

        def add_bias(g):
            sums = upool.tile([P, SIZES[g] * P], F32, tag="sums", name="sums")
            nc.scalar.activation(out=sums[:], in_=acc_tiles[g][:], func=ACT.Identity, bias=b_sb[:, 0:1], scale=1.0)
            sum_tiles[g] = sums

        def back_transposes(g):
            push = push_ps.tile([P, SIZES[g] * P], F32, tag="push", name="push")
            for j in range(SIZES[g]):
                nc.tensor.transpose(push[:, j * P:(j + 1) * P], sum_tiles[g][:, j * P:(j + 1) * P], ident[:])
            push_tiles[g] = push

        def stacks_of(g):
            c = g_chunk[g]
            entries = []
            for q in range(SIZES[g] * NS):
                lo = (g_start[g] - c_start[c]) * ROW + q * STACK
                s_q, o_q = s_tiles[c][:, lo:lo + STACK], o_tiles[c][:, lo:lo + STACK]
                entries.append((q, s_q, o_q, e_tiles[g][:, q * STACK:(q + 1) * STACK], g_start[g] * NL + q * NA))
            return entries

        def seed_lower_cells(g):
            c = g_chunk[g]
            if g == c_first[c]:
                o_tiles[c] = opool.tile([P, CHUNKS[c] * ROW], F32, tag="o", name="o_sb")
            e_tiles[g] = epool.tile([P, SIZES[g] * ROW], F32, tag="e", name="e_sb")
            for q, s_q, o_q, e_q, a_q in stacks_of(g):
                if g_start[g] < VECTOR_TILES:
                    nc.vector.tensor_scalar(
                        out=e_q[:, CS:STACK],
                        in0=s_q[:, 0:STACK - CS],
                        scalar1=act[:, a_q:a_q + 1],
                        scalar2=None,
                        op0=ALU.mult,
                    )
                else:
                    nc.scalar.activation(
                        out=e_q[:, CS:STACK], in_=s_q[:, 0:STACK - CS], func=ACT.Copy, scale=act[:, a_q:a_q + 1]
                    )

        def seed_top_cells_together(g):
            n_q = SIZES[g] * NS
            cells = e_tiles[g][:].rearrange("p (q x) -> p q x", x=STACK)
            a_lo = g_start[g] * NL
            weights = act[:, a_lo:a_lo + n_q * NA].rearrange("p (q a) -> p q a", a=NA)
            nc.vector.tensor_tensor(
                out=cells[:, :, 0:CS],
                in0=push_tiles[g][:].rearrange("p (q x) -> p q x", x=CS),
                in1=weights[:, :, 0:1].to_broadcast([P, n_q, CS]),
                op=ALU.mult,
            )

        def seed_top_cells(g):
            for q, s_q, o_q, e_q, a_q in stacks_of(g):
                nc.scalar.activation(
                    out=e_q[:, 0:CS], in_=push_tiles[g][:, q * CS:(q + 1) * CS], func=ACT.Copy, scale=act[:, a_q:a_q + 1]
                )

        def blend(g):
            entries = stacks_of(g)
            for j in range(SIZES[g]):
                for q, s_q, o_q, e_q, a_q in entries[j * NS:(j + 1) * NS]:
                    nc.vector.scalar_tensor_tensor(
                        out=o_q, in0=s_q, scalar=act[:, a_q + 2:a_q + 3], in1=e_q, op0=ALU.mult, op1=ALU.add
                    )
                for q, s_q, o_q, e_q, a_q in entries[j * NS:(j + 1) * NS]:
                    nc.vector.scalar_tensor_tensor(
                        out=o_q[:, 0:STACK - CS],
                        in0=s_q[:, CS:STACK],
                        scalar=act[:, a_q + 1:a_q + 2],
                        in1=o_q[:, 0:STACK - CS],
                        op0=ALU.mult,
                        op1=ALU.add,
                    )

        def store(g):
            c = g_chunk[g]
            t0, gt = g_start[g], SIZES[g]
            if c == n_chunks - 1:
                lo = (t0 - c_start[c]) * ROW
                pieces = 2 if g == n_groups - 1 else 1
                width = gt * ROW // pieces
                for i in range(pieces):
                    nc.sync.dma_start(
                        out=out_v[:, t0 * ROW + i * width:t0 * ROW + (i + 1) * width],
                        in_=o_tiles[c][:, lo + i * width:lo + (i + 1) * width],
                    )
            elif g == c_last[c]:
                nc.sync.dma_start(out=out_v[:, c_start[c] * ROW:(c_start[c] + CHUNKS[c]) * ROW], in_=o_tiles[c][:])
            if g == c_last[c] and c + LOAD_BUFS < n_chunks:
                load(c + LOAD_BUFS)

        softmax_max(0, HEAD_TILES)
        softmax_shift(0, HEAD_TILES)
        softmax_exp(0, HEAD_TILES)
        softmax_max(HEAD_TILES, TILES)
        softmax_sum(0, HEAD_TILES)
        softmax_norm(0, HEAD_TILES)
        softmax_shift(HEAD_TILES, TILES)

        w_grouped = const.tile([P, PASSES * P * PACK], BF16, align_bytes=64)
        copy_out(
            transpose_words(w_sb[:].bitcast(F32), 0),
            w_grouped[:].bitcast(F32).rearrange("p (m r u) -> p m r u", m=PASSES, u=2),
        )
        w_codes = const.tile([P, PASSES * P], U32, align_bytes=64)
        w_scales = const.tile([P, PASSES * P], U8, align_bytes=64)
        nc.vector.quantize_mx(out=w_codes[:].bitcast(FP8X4), scales=w_scales[:], in_=w_grouped[:])

        for k in range(-3, n_groups):
            if k >= 1:
                store(k - 1)
            if k + 3 < n_groups:
                transposes(k + 3)
            if 0 <= k + 1 < n_groups:
                add_bias(k + 1)
                back_transposes(k + 1)
            if k == -1:
                softmax_sum(HEAD_TILES, TILES)
            if 0 <= k + 2 < n_groups:
                if g_start[k + 2] < VECTOR_TILES:
                    seed_lower_cells(k + 2)
                quantise(k + 2)
                mx_passes(k + 2)
            if k == -2:
                softmax_exp(HEAD_TILES, TILES)
            if k == -1:
                softmax_norm(HEAD_TILES, TILES)
            if k + 3 < n_groups:
                copies_out(k + 3)
            if 0 <= k + 1 < n_groups and g_start[k + 1] >= VECTOR_TILES:
                seed_lower_cells(k + 1)
            if 0 <= k + 1 < n_groups and k + 1 != FIRST_PAIR:
                seed_top_cells(k + 1)
            if k >= 0:
                blend(k)
            if k + 1 == FIRST_PAIR:
                seed_top_cells_together(k + 1)
        store(n_groups - 1)
